import numpy as np
import ml_dtypes


def mxq(x, axis, fmt="e4m3"):
    dtype, down = {"e4m3": (ml_dtypes.float8_e4m3fn, 7), "e5m2": (ml_dtypes.float8_e5m2, 14)}[fmt]
    v = np.moveaxis(np.asarray(x, np.float32).astype(ml_dtypes.bfloat16).astype(np.float64), axis, -1)
    blocks = v.reshape(v.shape[:-1] + (-1, 32))
    amax = np.abs(blocks).max(-1, keepdims=True)
    byte = np.maximum(np.where(amax > 0, np.frexp(amax)[1] - 1 + 127, 0) - down, 1)
    scale = np.exp2(byte - 127.0)
    codes = (blocks / scale).astype(np.float32).astype(dtype).astype(np.float64)
    return np.moveaxis((codes * scale).reshape(v.shape), -1, axis)


WIDE = False


def mx_kscale(k):
    if not WIDE:
        return np.ones(k)
    levels = np.array([10, -10, 5, -5, 0])
    a = np.random.permutation(np.resize(levels, k // 512 * 4)).reshape(k // 512, 4)
    idx = np.arange(k)
    return np.exp2(a[idx // 512, idx % 128 // 32])


BF16 = ml_dtypes.bfloat16


def bf(x):
    return np.asarray(x, np.float32).astype(BF16)


def f64(x):
    return np.asarray(x).astype(np.float64)


B, D, R, P = 8192, 512, 128, 3


def draw_u(s):
    return bf(np.random.standard_normal((D, R)) / np.sqrt(D) / s[:, None])


def setup_inputs():
    s = mx_kscale(D)
    return {"X": bf(np.random.standard_normal((B, D)) * s),
            "U_0_0": draw_u(s), "U_1_0": draw_u(s), "U_1_1": draw_u(s),
            "U_2_0": draw_u(s), "U_2_1": draw_u(s), "U_2_2": draw_u(s),
            "C": bf((1.0 + 0.25 * np.random.standard_normal(P)) / np.sqrt(R)),
            "beta": bf(1.0 + 0.25 * np.random.standard_normal(1))}


def reference(X, U_0_0, U_1_0, U_1_1, U_2_0, U_2_1, U_2_2, C, beta):
    xq = mxq(f64(X).reshape(B, D), 1, "e4m3")
    c = f64(C)
    u_lists = [[U_0_0], [U_1_0, U_1_1], [U_2_0, U_2_1, U_2_2]]
    preds = f64(beta)[0]
    for j, u_j in enumerate(u_lists):
        prod = None
        for u in u_j:
            dot = xq @ mxq(f64(u), 0, "e4m3")
            prod = dot if prod is None else prod * dot
        preds = preds + c[j] * np.sum(prod, axis=1)
    return preds

@@ -1,0 +1,272 @@
+from contextlib import ExitStack
+
+import concourse.mybir as mybir
+from concourse.masks import make_identity
+
+FP8X4 = mybir.dt.float8_e4m3fn_x4
+BF16 = mybir.dt.bfloat16
+F32 = mybir.dt.float32
+U32 = mybir.dt.uint32
+U8 = mybir.dt.uint8
+MULT = mybir.AluOpType.mult
+ADD = mybir.AluOpType.add
+COPY = mybir.ActivationFunctionType.Copy
+
+B, D, R = 8192, 512, 128
+P = 128
+TILES = B // P
+PAIRS = TILES // 2
+FLOPS = 2 * B * D * R * 6
+CHUNKS = (2, 2, 4, 8, 8, 8, 8, 8, 8, 8)
+AHEAD = 4
+
+
+def tile_polynomialtensorregression_pa_t_kernel(
+    tc, X, U_0_0, U_1_0, U_1_1, U_2_0, U_2_1, U_2_2, C, beta, out
+):
+    nc = tc.nc
+    with ExitStack() as ctx:
+        keep = ctx.enter_context(tc.tile_pool(name="keep", bufs=1))
+        work = ctx.enter_context(tc.tile_pool(name="work", bufs=3))
+        psum = ctx.enter_context(tc.psum_pool(name="psum", bufs=2))
+        ctx.enter_context(tc.manual_schedule())
+
+        ident = keep.tile([P, P], F32, name="ident")
+        make_identity(nc, ident[:])
+        warm = keep.tile([P, 1], F32, name="warm")
+        warm2 = keep.tile([P, 1], F32, name="warm2")
+        nc.vector.memset(warm[:], 0.0)
+        nc.scalar.activation(out=warm2[:], in_=warm[:], func=COPY)
+
+        c_bf = keep.tile([P, 3], BF16, name="c_bf")
+        b_bf = keep.tile([P, 1], BF16, name="b_bf")
+        nc.scalar.dma_start(out=c_bf[:], in_=C.partition_broadcast(P))
+        nc.scalar.dma_start(out=b_bf[:], in_=beta.partition_broadcast(P))
+
+        x_view = X.rearrange("(p t) k -> p t k", t=TILES)
+        x_of = []
+        x_chunks = []
+        first = 0
+        for c, n in enumerate(CHUNKS):
+            x_sb = keep.tile([P, n, D], BF16, name="x%d" % c)
+            x_chunks.append((x_sb, first, n))
+            for i in range(n):
+                x_of.append((x_sb, i))
+            first += n
+
+        def load_x(c):
+            x_sb, t0, n = x_chunks[c]
+            nc.sync.dma_start(out=x_sb[:], in_=x_view[:, t0 : t0 + n, :])
+
+        u_order = (U_1_0, U_2_0, U_2_1, U_0_0, U_1_1, U_2_2)
+        u_raw = []
+        load_x(0)
+        for i, u_dram in enumerate(u_order):
+            raw = keep.tile([P, D], BF16, name="u_raw%d" % i)
+            u_raw.append(raw)
+            nc.sync.dma_start(
+                out=raw[:].rearrange("p (u e c) -> p u e c", u=2, e=2),
+                in_=u_dram.rearrange("(u q e) c -> q u e c", u=2, e=2),
+            )
+        for c in range(1, len(CHUNKS)):
+            load_x(c)
+
+        u_grp = []
+        u_codes = []
+        u_scales = []
+        for pr in range(3):
+            u_grp.append(keep.tile([P, 2 * D], BF16, name="u_grp%d" % pr, align_bytes=64))
+            u_codes.append(keep.tile([P, 2 * R], U32, name="u_codes%d" % pr, align_bytes=64))
+            u_scales.append(keep.tile([P, 2 * R], U8, name="u_scales%d" % pr, align_bytes=64))
+        x_codes = []
+        x_scales = []
+        for g in range(PAIRS // 2):
+            x_codes.append(keep.tile([P, 4 * P], U32, name="x_codes%d" % g, align_bytes=64))
+            x_scales.append(keep.tile([P, 4 * P], U8, name="x_scales%d" % g, align_bytes=64))
+        c_f = keep.tile([P, 3], F32, name="c_f")
+        b_f = keep.tile([P, 1], F32, name="b_f")
+        s0 = keep.tile([P, TILES], F32, name="s0")
+        s1 = keep.tile([P, TILES], F32, name="s1")
+        s2 = keep.tile([P, TILES], F32, name="s2")
+        junk_s = keep.tile([P, R], F32, name="junk_s")
+        junk_v = keep.tile([P, R], F32, name="junk_v")
+        part = keep.tile([P, TILES], F32, name="part")
+        res = keep.tile([P, TILES], F32, name="res")
+
+        def regroup_u(i):
+            nc.vector.tensor_copy(
+                out=u_grp[i // 2][:, (i % 2) * D : (i % 2 + 1) * D].rearrange(
+                    "p (c i t) -> p c t i", i=4, t=4
+                ),
+                in_=u_raw[i][:].rearrange("p (t c i) -> p c t i", t=4, i=4),
+            )
+
+        def quantise_u(pr):
+            nc.vector.quantize_mx(
+                out=u_codes[pr][:].bitcast(FP8X4), scales=u_scales[pr][:], in_=u_grp[pr][:]
+            )
+
+        xts = {}
+        groupeds = {}
+
+        def transposes(j):
+            xt = psum.tile([P, 512], F32, name="xt")
+            xts[j] = xt
+            for s in range(2):
+                x_sb, i = x_of[2 * j + s]
+                words = x_sb[:, i, :].bitcast(F32)
+                for u in range(2):
+                    col = (2 * s + u) * P
+                    nc.tensor.transpose(
+                        xt[:, col : col + P], words[:, u * P : (u + 1) * P], ident[:]
+                    )
+
+        def copy_xt(j):
+            if j % 2 == 0:
+                grouped = work.tile([P, 2048], BF16, name="grouped", align_bytes=64, bufs=4)
+                groupeds[j // 2] = grouped
+            half = j % 2
+            nc.scalar.copy(
+                out=groupeds[j // 2][:, half * 1024 : (half + 1) * 1024]
+                .bitcast(F32)
+                .rearrange("p (s b u) -> p s b u", s=2, u=2),
+                in_=xts[j][:].rearrange("p (s u b) -> p s b u", s=2, u=2),
+            )
+
+        def quantise_x(j0, n):
+            g = j0 // 2
+            half = j0 % 2
+            nc.vector.quantize_mx(
+                out=x_codes[g][:, half * 256 : (half + n) * 256].bitcast(FP8X4),
+                scales=x_scales[g][:, half * 256 : (half + n) * 256],
+                in_=groupeds[g][:, half * 1024 : (half + n) * 1024],
+            )
+
+        banks = {}
+
+        def mx(j):
+            p_bank = psum.tile([P, 512], F32, name="p_bank")
+            r_bank = psum.tile([P, 512], F32, name="r_bank")
+            q_bank = psum.tile([P, 512], F32, name="q_bank")
+            banks[j] = (p_bank, r_bank, q_bank)
+            for pr in range(3):
+                for s in range(2):
+                    col = ((2 * j + s) % 4) * P
+                    nc.tensor.matmul_mx(
+                        out=banks[j][pr][:, s * 256 : (s + 1) * 256],
+                        lhsT=x_codes[j // 2][:, col : col + P].bitcast(FP8X4),
+                        lhsT_scale=x_scales[j // 2][:, col : col + P],
+                        rhs=u_codes[pr][:].bitcast(FP8X4),
+                        rhs_scale=u_scales[pr][:],
+                        start=True,
+                        stop=True,
+                    )
+
+        a_tiles = {}
+
+        def scalar_part(j):
+            p_bank, r_bank, q_bank = banks[j]
+            a = work.tile([P, 512], F32, name="a")
+            a_tiles[j] = a
+            nc.scalar.copy(out=a[:], in_=p_bank[:])
+            for s in range(2):
+                t = 2 * j + s
+                nc.scalar.activation(
+                    out=junk_s[:],
+                    in_=r_bank[:, s * 256 + 128 : (s + 1) * 256],
+                    func=COPY,
+                    accum_out=s0[:, t : t + 1],
+                )
+
+        def vector_part(j):
+            p_bank, r_bank, q_bank = banks[j]
+            a = a_tiles[j]
+            for s in range(2):
+                t = 2 * j + s
+                nc.vector.scalar_tensor_tensor(
+                    out=junk_v[:],
+                    in0=a[:, s * 256 : s * 256 + 128],
+                    scalar=c_f[:, 1:2],
+                    in1=q_bank[:, s * 256 : s * 256 + 128],
+                    op0=MULT,
+                    op1=MULT,
+                    accum_out=s1[:, t : t + 1],
+                )
+            h = work.tile([P, 256], F32, name="h")
+            nc.vector.tensor_tensor(
+                out=h[:].rearrange("p (s r) -> p s r", s=2),
+                in0=a[:].rearrange("p (s c) -> p s c", s=2)[:, :, 128:256],
+                in1=r_bank[:].rearrange("p (s c) -> p s c", s=2)[:, :, 0:128],
+                op=MULT,
+            )
+            if j == PAIRS - 1:
+                nc.vector.tensor_scalar(
+                    out=part[:],
+                    in0=s0[:],
+                    scalar1=c_f[:, 0:1],
+                    scalar2=b_f[:, 0:1],
+                    op0=MULT,
+                    op1=ADD,
+                )
+                nc.vector.tensor_tensor(out=part[:], in0=part[:], in1=s1[:], op=ADD)
+            for s in range(2):
+                t = 2 * j + s
+                nc.vector.scalar_tensor_tensor(
+                    out=junk_v[:],
+                    in0=h[:, s * 128 : (s + 1) * 128],
+                    scalar=c_f[:, 2:3],
+                    in1=q_bank[:, s * 256 + 128 : (s + 1) * 256],
+                    op0=MULT,
+                    op1=MULT,
+                    accum_out=s2[:, t : t + 1],
+                )
+
+        transposes(0)
+        copy_xt(0)
+        regroup_u(0)
+        regroup_u(1)
+        quantise_x(0, 1)
+        regroup_u(2)
+        regroup_u(3)
+        quantise_u(0)
+        regroup_u(4)
+        quantise_u(1)
+        regroup_u(5)
+        quantise_u(2)
+        nc.vector.tensor_copy(out=c_f[:], in_=c_bf[:])
+        nc.vector.tensor_copy(out=b_f[:], in_=b_bf[:])
+        transposes(1)
+        copy_xt(1)
+
+        mx(0)
+        transposes(2)
+        transposes(3)
+        scalar_part(0)
+        copy_xt(2)
+        copy_xt(3)
+        quantise_x(1, 1)
+        vector_part(0)
+        quantise_x(2, 2)
+
+        mx(1)
+        transposes(4)
+        transposes(5)
+        scalar_part(1)
+        copy_xt(4)
+        copy_xt(5)
+        vector_part(1)
+
+        for j in range(2, PAIRS):
+            mx(j)
+            if j % 2 == 0 and j + AHEAD < PAIRS:
+                transposes(j + AHEAD)
+                transposes(j + AHEAD + 1)
+            scalar_part(j)
+            if j + AHEAD < PAIRS:
+                copy_xt(j + AHEAD)
+            if j % 2 == 0 and j + 2 < PAIRS:
+                quantise_x(j + 2, 2)
+            vector_part(j)
+
+        nc.vector.tensor_tensor(out=res[:], in0=part[:], in1=s2[:], op=ADD)
+        nc.sync.dma_start(out=out.rearrange("(p t) -> p t", t=TILES), in_=res[:])

@@ -88,9 +88,8 @@ def tile_polynomialtensorregression_pa_t_kernel(
         s0 = keep.tile([P, TILES], F32, name="s0")
         s1 = keep.tile([P, TILES], F32, name="s1")
         s2 = keep.tile([P, TILES], F32, name="s2")
-        junk_s = keep.tile([P, R], F32, name="junk_s")
-        junk_v = keep.tile([P, R], F32, name="junk_v")
         part = keep.tile([P, TILES], F32, name="part")
+        part2 = keep.tile([P, TILES], F32, name="part2")
         res = keep.tile([P, TILES], F32, name="res")
 
         def regroup_u(i):
@@ -171,6 +170,7 @@ def tile_polynomialtensorregression_pa_t_kernel(
             nc.scalar.copy(out=a[:], in_=p_bank[:])
             for s in range(2):
                 t = 2 * j + s
+                junk_s = work.tile([P, R], F32, name="junk_s", bufs=4)
                 nc.scalar.activation(
                     out=junk_s[:],
                     in_=r_bank[:, s * 256 + 128 : (s + 1) * 256],
@@ -181,8 +181,16 @@ def tile_polynomialtensorregression_pa_t_kernel(
         def vector_part(j):
             p_bank, r_bank, q_bank = banks[j]
             a = a_tiles[j]
+            h = work.tile([P, 256], F32, name="h")
+            nc.vector.tensor_tensor(
+                out=h[:].rearrange("p (s r) -> p s r", s=2),
+                in0=a[:].rearrange("p (s c) -> p s c", s=2)[:, :, 128:256],
+                in1=r_bank[:].rearrange("p (s c) -> p s c", s=2)[:, :, 0:128],
+                op=MULT,
+            )
             for s in range(2):
                 t = 2 * j + s
+                junk_v = work.tile([P, R], F32, name="junk_v", bufs=6)
                 nc.vector.scalar_tensor_tensor(
                     out=junk_v[:],
                     in0=a[:, s * 256 : s * 256 + 128],
@@ -192,13 +200,6 @@ def tile_polynomialtensorregression_pa_t_kernel(
                     op1=MULT,
                     accum_out=s1[:, t : t + 1],
                 )
-            h = work.tile([P, 256], F32, name="h")
-            nc.vector.tensor_tensor(
-                out=h[:].rearrange("p (s r) -> p s r", s=2),
-                in0=a[:].rearrange("p (s c) -> p s c", s=2)[:, :, 128:256],
-                in1=r_bank[:].rearrange("p (s c) -> p s c", s=2)[:, :, 0:128],
-                op=MULT,
-            )
             if j == PAIRS - 1:
                 nc.vector.tensor_scalar(
                     out=part[:],
@@ -208,9 +209,9 @@ def tile_polynomialtensorregression_pa_t_kernel(
                     op0=MULT,
                     op1=ADD,
                 )
-                nc.vector.tensor_tensor(out=part[:], in0=part[:], in1=s1[:], op=ADD)
             for s in range(2):
                 t = 2 * j + s
+                junk_v = work.tile([P, R], F32, name="junk_v", bufs=6)
                 nc.vector.scalar_tensor_tensor(
                     out=junk_v[:],
                     in0=h[:, s * 128 : (s + 1) * 128],
@@ -220,6 +221,8 @@ def tile_polynomialtensorregression_pa_t_kernel(
                     op1=MULT,
                     accum_out=s2[:, t : t + 1],
                 )
+                if j == PAIRS - 1 and s == 0:
+                    nc.vector.tensor_tensor(out=part2[:], in0=part[:], in1=s1[:], op=ADD)
 
         transposes(0)
         copy_xt(0)
@@ -268,5 +271,5 @@ def tile_polynomialtensorregression_pa_t_kernel(
                 quantise_x(j + 2, 2)
             vector_part(j)
 
-        nc.vector.tensor_tensor(out=res[:], in0=part[:], in1=s2[:], op=ADD)
+        nc.vector.tensor_tensor(out=res[:], in0=part2[:], in1=s2[:], op=ADD)
         nc.sync.dma_start(out=out.rearrange("(p t) -> p t", t=TILES), in_=res[:])

@@ -18,7 +18,16 @@ TILES = B // P
 PAIRS = TILES // 2
 FLOPS = 2 * B * D * R * 6
 CHUNKS = (2, 2, 4, 8, 8, 8, 8, 8, 8, 8)
-AHEAD = 4
+RAMP = 4
+FIN_BUFS = 3
+
+
+def d0_on_scalar(t):
+    if t < 8:
+        return t % 2 == 0
+    if t >= 52:
+        return True
+    return t % 4 != 3
 
 
 def tile_polynomialtensorregression_pa_t_kernel(
@@ -58,26 +67,33 @@ def tile_polynomialtensorregression_pa_t_kernel(
             x_sb, t0, n = x_chunks[c]
             nc.sync.dma_start(out=x_sb[:], in_=x_view[:, t0 : t0 + n, :])
 
-        u_order = (U_1_0, U_2_0, U_2_1, U_0_0, U_1_1, U_2_2)
+        u_order = (U_1_0, U_2_0, U_2_1, U_1_1, U_0_0, U_2_2)
         u_raw = []
-        load_x(0)
-        for i, u_dram in enumerate(u_order):
+
+        def load_u(i):
             raw = keep.tile([P, D], BF16, name="u_raw%d" % i)
             u_raw.append(raw)
             nc.sync.dma_start(
                 out=raw[:].rearrange("p (u e c) -> p u e c", u=2, e=2),
-                in_=u_dram.rearrange("(u q e) c -> q u e c", u=2, e=2),
+                in_=u_order[i].rearrange("(u q e) c -> q u e c", u=2, e=2),
             )
-        for c in range(1, len(CHUNKS)):
+
+        load_x(0)
+        load_u(0)
+        load_u(1)
+        load_x(1)
+        for i in range(2, 6):
+            load_u(i)
+        for c in range(2, len(CHUNKS)):
             load_x(c)
 
         u_grp = []
-        u_codes = []
-        u_scales = []
-        for pr in range(3):
-            u_grp.append(keep.tile([P, 2 * D], BF16, name="u_grp%d" % pr, align_bytes=64))
-            u_codes.append(keep.tile([P, 2 * R], U32, name="u_codes%d" % pr, align_bytes=64))
-            u_scales.append(keep.tile([P, 2 * R], U8, name="u_scales%d" % pr, align_bytes=64))
+        for n in range(3):
+            u_grp.append(keep.tile([P, 2 * D], BF16, name="u_grp%d" % n, align_bytes=64))
+        up_codes = keep.tile([P, 2 * R], U32, name="up_codes", align_bytes=64)
+        up_scales = keep.tile([P, 2 * R], U8, name="up_scales", align_bytes=64)
+        uq_codes = keep.tile([P, 4 * R], U32, name="uq_codes", align_bytes=64)
+        uq_scales = keep.tile([P, 4 * R], U8, name="uq_scales", align_bytes=64)
         x_codes = []
         x_scales = []
         for g in range(PAIRS // 2):
@@ -86,11 +102,15 @@ def tile_polynomialtensorregression_pa_t_kernel(
         c_f = keep.tile([P, 3], F32, name="c_f")
         b_f = keep.tile([P, 1], F32, name="b_f")
         s0 = keep.tile([P, TILES], F32, name="s0")
-        s1 = keep.tile([P, TILES], F32, name="s1")
-        s2 = keep.tile([P, TILES], F32, name="s2")
+        acc = keep.tile([P, TILES], F32, name="acc")
         part = keep.tile([P, TILES], F32, name="part")
-        part2 = keep.tile([P, TILES], F32, name="part2")
         res = keep.tile([P, TILES], F32, name="res")
+        fins = []
+        for n in range(FIN_BUFS):
+            fin = keep.tile([P, 2, 3, R], F32, name="fin%d" % n)
+            fins.append(fin)
+            nc.vector.memset(fin[:, :, 1, :], 1.0)
+        nc.vector.memset(s0[:], 0.0)
 
         def regroup_u(i):
             nc.vector.tensor_copy(
@@ -100,10 +120,25 @@ def tile_polynomialtensorregression_pa_t_kernel(
                 in_=u_raw[i][:].rearrange("p (t c i) -> p c t i", t=4, i=4),
             )
 
-        def quantise_u(pr):
-            nc.vector.quantize_mx(
-                out=u_codes[pr][:].bitcast(FP8X4), scales=u_scales[pr][:], in_=u_grp[pr][:]
-            )
+        def quantise_u(i):
+            if i == 0:
+                codes, scales = up_codes[:], up_scales[:]
+            else:
+                codes = uq_codes[:, (i - 2) * R : i * R]
+                scales = uq_scales[:, (i - 2) * R : i * R]
+            nc.vector.quantize_mx(out=codes.bitcast(FP8X4), scales=scales, in_=u_grp[i // 2][:])
+
+        def constants():
+            nc.vector.tensor_copy(out=c_f[:], in_=c_bf[:])
+            nc.vector.tensor_copy(out=b_f[:], in_=b_bf[:])
+            for fin in fins:
+                nc.vector.tensor_scalar(
+                    out=fin[:, :, 1, :],
+                    in0=fin[:, :, 1, :],
+                    scalar1=c_f[:, 0:1],
+                    scalar2=None,
+                    op0=MULT,
+                )
 
         xts = {}
         groupeds = {}
@@ -141,135 +176,141 @@ def tile_polynomialtensorregression_pa_t_kernel(
                 in_=groupeds[g][:, half * 1024 : (half + n) * 1024],
             )
 
-        banks = {}
+        pbs = {}
+        qbs = {}
 
         def mx(j):
-            p_bank = psum.tile([P, 512], F32, name="p_bank")
-            r_bank = psum.tile([P, 512], F32, name="r_bank")
-            q_bank = psum.tile([P, 512], F32, name="q_bank")
-            banks[j] = (p_bank, r_bank, q_bank)
-            for pr in range(3):
-                for s in range(2):
-                    col = ((2 * j + s) % 4) * P
-                    nc.tensor.matmul_mx(
-                        out=banks[j][pr][:, s * 256 : (s + 1) * 256],
-                        lhsT=x_codes[j // 2][:, col : col + P].bitcast(FP8X4),
-                        lhsT_scale=x_scales[j // 2][:, col : col + P],
-                        rhs=u_codes[pr][:].bitcast(FP8X4),
-                        rhs_scale=u_scales[pr][:],
-                        start=True,
-                        stop=True,
+            pb = psum.tile([P, 512], F32, name="pb")
+            pbs[j] = pb
+            for s in range(2):
+                col = ((2 * j + s) % 4) * P
+                nc.tensor.matmul_mx(
+                    out=pb[:, s * 256 : (s + 1) * 256],
+                    lhsT=x_codes[j // 2][:, col : col + P].bitcast(FP8X4),
+                    lhsT_scale=x_scales[j // 2][:, col : col + P],
+                    rhs=up_codes[:].bitcast(FP8X4),
+                    rhs_scale=up_scales[:],
+                    start=True,
+                    stop=True,
+                )
+            for s in range(2):
+                col = ((2 * j + s) % 4) * P
+                qb = psum.tile([P, 512], F32, name="qb", bufs=4)
+                qbs[2 * j + s] = qb
+                nc.tensor.matmul_mx(
+                    out=qb[:],
+                    lhsT=x_codes[j // 2][:, col : col + P].bitcast(FP8X4),
+                    lhsT_scale=x_scales[j // 2][:, col : col + P],
+                    rhs=uq_codes[:].bitcast(FP8X4),
+                    rhs_scale=uq_scales[:],
+                    start=True,
+                    stop=True,
+                )
+
+        a3s = {}
+
+        def copies(j):
+            pb = pbs[j][:].rearrange("p (s c) -> p s c", s=2)
+            a3 = work.tile([P, 2, R], F32, name="a3")
+            a3s[j] = a3
+            nc.scalar.copy(out=a3[:], in_=pb[:, :, 128:256])
+            nc.scalar.activation(
+                out=fins[j % FIN_BUFS][:, :, 0, :], in_=pb[:, :, 0:128], func=COPY, scale=c_f[:, 1:2]
+            )
+
+        def linear_sums(j):
+            for t in (2 * j, 2 * j + 1):
+                if d0_on_scalar(t):
+                    junk_s = work.tile([P, R], F32, name="junk_s", bufs=4)
+                    nc.scalar.activation(
+                        out=junk_s[:], in_=qbs[t][:, 256:384], func=COPY, accum_out=s0[:, t : t + 1]
                     )
 
-        a_tiles = {}
-
-        def scalar_part(j):
-            p_bank, r_bank, q_bank = banks[j]
-            a = work.tile([P, 512], F32, name="a")
-            a_tiles[j] = a
-            nc.scalar.copy(out=a[:], in_=p_bank[:])
-            for s in range(2):
-                t = 2 * j + s
-                junk_s = work.tile([P, R], F32, name="junk_s", bufs=4)
-                nc.scalar.activation(
-                    out=junk_s[:],
-                    in_=r_bank[:, s * 256 + 128 : (s + 1) * 256],
-                    func=COPY,
-                    accum_out=s0[:, t : t + 1],
-                )
-
         def vector_part(j):
-            p_bank, r_bank, q_bank = banks[j]
-            a = a_tiles[j]
-            h = work.tile([P, 256], F32, name="h")
-            nc.vector.tensor_tensor(
-                out=h[:].rearrange("p (s r) -> p s r", s=2),
-                in0=a[:].rearrange("p (s c) -> p s c", s=2)[:, :, 128:256],
-                in1=r_bank[:].rearrange("p (s c) -> p s c", s=2)[:, :, 0:128],
-                op=MULT,
-            )
+            fin = fins[j % FIN_BUFS]
             for s in range(2):
-                t = 2 * j + s
-                junk_v = work.tile([P, R], F32, name="junk_v", bufs=6)
                 nc.vector.scalar_tensor_tensor(
-                    out=junk_v[:],
-                    in0=a[:, s * 256 : s * 256 + 128],
-                    scalar=c_f[:, 1:2],
-                    in1=q_bank[:, s * 256 : s * 256 + 128],
-                    op0=MULT,
-                    op1=MULT,
-                    accum_out=s1[:, t : t + 1],
-                )
-            if j == PAIRS - 1:
-                nc.vector.tensor_scalar(
-                    out=part[:],
-                    in0=s0[:],
-                    scalar1=c_f[:, 0:1],
-                    scalar2=b_f[:, 0:1],
-                    op0=MULT,
-                    op1=ADD,
-                )
-            for s in range(2):
-                t = 2 * j + s
-                junk_v = work.tile([P, R], F32, name="junk_v", bufs=6)
-                nc.vector.scalar_tensor_tensor(
-                    out=junk_v[:],
-                    in0=h[:, s * 128 : (s + 1) * 128],
+                    out=fin[:, s, 2, :],
+                    in0=a3s[j][:, s, :],
                     scalar=c_f[:, 2:3],
-                    in1=q_bank[:, s * 256 + 128 : (s + 1) * 256],
+                    in1=qbs[2 * j + s][:, 0:128],
                     op0=MULT,
                     op1=MULT,
-                    accum_out=s2[:, t : t + 1],
                 )
-                if j == PAIRS - 1 and s == 0:
-                    nc.vector.tensor_tensor(out=part2[:], in0=part[:], in1=s1[:], op=ADD)
+            for s in range(2):
+                t = 2 * j + s
+                if t == TILES - 1:
+                    nc.vector.tensor_scalar(
+                        out=part[:],
+                        in0=s0[:],
+                        scalar1=c_f[:, 0:1],
+                        scalar2=b_f[:, 0:1],
+                        op0=MULT,
+                        op1=ADD,
+                    )
+                junk_v = work.tile([P, 3, R], F32, name="junk_v", bufs=4)
+                rest = qbs[t][:, 128:512].rearrange("p (b r) -> p b r", b=3)
+                if d0_on_scalar(t):
+                    nc.vector.scalar_tensor_tensor(
+                        out=junk_v[:, 0:2, :],
+                        in0=fin[:, s, 0:3:2, :],
+                        scalar=1.0,
+                        in1=rest[:, 0:3:2, :],
+                        op0=MULT,
+                        op1=MULT,
+                        accum_out=acc[:, t : t + 1],
+                    )
+                else:
+                    nc.vector.scalar_tensor_tensor(
+                        out=junk_v[:],
+                        in0=fin[:, s, :, :],
+                        scalar=1.0,
+                        in1=rest,
+                        op0=MULT,
+                        op1=MULT,
+                        accum_out=acc[:, t : t + 1],
+                    )
 
         transposes(0)
         copy_xt(0)
         regroup_u(0)
         regroup_u(1)
-        quantise_x(0, 1)
-        regroup_u(2)
-        regroup_u(3)
         quantise_u(0)
-        regroup_u(4)
-        quantise_u(1)
-        regroup_u(5)
-        quantise_u(2)
-        nc.vector.tensor_copy(out=c_f[:], in_=c_bf[:])
-        nc.vector.tensor_copy(out=b_f[:], in_=b_bf[:])
+        constants()
+        quantise_x(0, 1)
         transposes(1)
         copy_xt(1)
-
-        mx(0)
-        transposes(2)
-        transposes(3)
-        scalar_part(0)
-        copy_xt(2)
-        copy_xt(3)
+        regroup_u(2)
+        regroup_u(3)
+        quantise_u(2)
         quantise_x(1, 1)
-        vector_part(0)
-        quantise_x(2, 2)
+        regroup_u(4)
+        regroup_u(5)
+        quantise_u(4)
 
-        mx(1)
-        transposes(4)
-        transposes(5)
-        scalar_part(1)
-        copy_xt(4)
-        copy_xt(5)
-        vector_part(1)
+        done = {"transposed": 2, "copied": 2, "quantised": 2}
 
-        for j in range(2, PAIRS):
+        def copy_one():
+            if done["copied"] < done["transposed"]:
+                copy_xt(done["copied"])
+                done["copied"] += 1
+
+        for j in range(PAIRS):
+            copy_one()
             mx(j)
-            if j % 2 == 0 and j + AHEAD < PAIRS:
-                transposes(j + AHEAD)
-                transposes(j + AHEAD + 1)
-            scalar_part(j)
-            if j + AHEAD < PAIRS:
-                copy_xt(j + AHEAD)
-            if j % 2 == 0 and j + 2 < PAIRS:
-                quantise_x(j + 2, 2)
+            copies(j)
+            copy_one()
+            linear_sums(j)
             vector_part(j)
+            if done["quantised"] + 2 <= done["copied"]:
+                quantise_x(done["quantised"], 2)
+                done["quantised"] += 2
+            if (j < RAMP or j % 2 == 1) and done["transposed"] < PAIRS:
+                copy_one()
+                copy_one()
+                transposes(done["transposed"])
+                transposes(done["transposed"] + 1)
+                done["transposed"] += 2
 
-        nc.vector.tensor_tensor(out=res[:], in0=part2[:], in1=s2[:], op=ADD)
+        nc.vector.tensor_tensor(out=res[:], in0=part[:], in1=acc[:], op=ADD)
         nc.sync.dma_start(out=out.rearrange("(p t) -> p t", t=TILES), in_=res[:])

@@ -16,18 +16,17 @@ B, D, R = 8192, 512, 128
 P = 128
 TILES = B // P
 PAIRS = TILES // 2
+ROUNDS = TILES // 4
 FLOPS = 2 * B * D * R * 6
-CHUNKS = (2, 2, 4, 8, 8, 8, 8, 8, 8, 8)
-RAMP = 4
-FIN_BUFS = 3
+CHUNKS = (2, 2, 4, 4, 4, 8, 8, 8, 8, 8, 8)
+X_LEAD = 3
+Q_LEAD = 2
+S_LEAD = 1
+FIN_BUFS = 6
 
 
 def d0_on_scalar(t):
-    if t < 8:
-        return t % 2 == 0
-    if t >= 52:
-        return True
-    return t % 4 != 3
+    return t >= 48 or t % 4 != 3
 
 
 def tile_polynomialtensorregression_pa_t_kernel(
@@ -36,8 +35,8 @@ def tile_polynomialtensorregression_pa_t_kernel(
     nc = tc.nc
     with ExitStack() as ctx:
         keep = ctx.enter_context(tc.tile_pool(name="keep", bufs=1))
-        work = ctx.enter_context(tc.tile_pool(name="work", bufs=3))
-        psum = ctx.enter_context(tc.psum_pool(name="psum", bufs=2))
+        work = ctx.enter_context(tc.tile_pool(name="work", bufs=4))
+        psum = ctx.enter_context(tc.psum_pool(name="psum", bufs=4))
         ctx.enter_context(tc.manual_schedule())
 
         ident = keep.tile([P, P], F32, name="ident")
@@ -67,7 +66,7 @@ def tile_polynomialtensorregression_pa_t_kernel(
             x_sb, t0, n = x_chunks[c]
             nc.sync.dma_start(out=x_sb[:], in_=x_view[:, t0 : t0 + n, :])
 
-        u_order = (U_1_0, U_2_0, U_2_1, U_1_1, U_0_0, U_2_2)
+        u_order = (U_1_0, U_2_0, U_0_0, U_1_1, U_2_2, U_2_1)
         u_raw = []
 
         def load_u(i):
@@ -96,7 +95,7 @@ def tile_polynomialtensorregression_pa_t_kernel(
         uq_scales = keep.tile([P, 4 * R], U8, name="uq_scales", align_bytes=64)
         x_codes = []
         x_scales = []
-        for g in range(PAIRS // 2):
+        for g in range(ROUNDS):
             x_codes.append(keep.tile([P, 4 * P], U32, name="x_codes%d" % g, align_bytes=64))
             x_scales.append(keep.tile([P, 4 * P], U8, name="x_scales%d" % g, align_bytes=64))
         c_f = keep.tile([P, 3], F32, name="c_f")
@@ -106,10 +105,12 @@ def tile_polynomialtensorregression_pa_t_kernel(
         part = keep.tile([P, TILES], F32, name="part")
         res = keep.tile([P, TILES], F32, name="res")
         fins = []
+        a3s = []
         for n in range(FIN_BUFS):
             fin = keep.tile([P, 2, 3, R], F32, name="fin%d" % n)
             fins.append(fin)
-            nc.vector.memset(fin[:, :, 1, :], 1.0)
+            nc.vector.memset(fin[:, :, 0, :], 1.0)
+            a3s.append(keep.tile([P, 2, R], F32, name="a3_%d" % n))
         nc.vector.memset(s0[:], 0.0)
 
         def regroup_u(i):
@@ -133,18 +134,30 @@ def tile_polynomialtensorregression_pa_t_kernel(
             nc.vector.tensor_copy(out=b_f[:], in_=b_bf[:])
             for fin in fins:
                 nc.vector.tensor_scalar(
-                    out=fin[:, :, 1, :],
-                    in0=fin[:, :, 1, :],
+                    out=fin[:, :, 0, :],
+                    in0=fin[:, :, 0, :],
                     scalar1=c_f[:, 0:1],
                     scalar2=None,
                     op0=MULT,
                 )
 
+        def mx(bank, t, codes, scales):
+            col = (t % 4) * P
+            nc.tensor.matmul_mx(
+                out=bank,
+                lhsT=x_codes[t // 4][:, col : col + P].bitcast(FP8X4),
+                lhsT_scale=x_scales[t // 4][:, col : col + P],
+                rhs=codes.bitcast(FP8X4),
+                rhs_scale=scales,
+                start=True,
+                stop=True,
+            )
+
         xts = {}
         groupeds = {}
 
         def transposes(j):
-            xt = psum.tile([P, 512], F32, name="xt")
+            xt = psum.tile([P, 512], F32, name="xt", tag="for_scalar")
             xts[j] = xt
             for s in range(2):
                 x_sb, i = x_of[2 * j + s]
@@ -157,7 +170,7 @@ def tile_polynomialtensorregression_pa_t_kernel(
 
         def copy_xt(j):
             if j % 2 == 0:
-                grouped = work.tile([P, 2048], BF16, name="grouped", align_bytes=64, bufs=4)
+                grouped = work.tile([P, 2048], BF16, name="grouped", align_bytes=64)
                 groupeds[j // 2] = grouped
             half = j % 2
             nc.scalar.copy(
@@ -167,79 +180,128 @@ def tile_polynomialtensorregression_pa_t_kernel(
                 in_=xts[j][:].rearrange("p (s u b) -> p s b u", s=2, u=2),
             )
 
-        def quantise_x(j0, n):
-            g = j0 // 2
-            half = j0 % 2
+        def quantise_x(g):
             nc.vector.quantize_mx(
-                out=x_codes[g][:, half * 256 : (half + n) * 256].bitcast(FP8X4),
-                scales=x_scales[g][:, half * 256 : (half + n) * 256],
-                in_=groupeds[g][:, half * 1024 : (half + n) * 1024],
+                out=x_codes[g][:].bitcast(FP8X4), scales=x_scales[g][:], in_=groupeds[g][:]
             )
 
         pbs = {}
+        dbs = {}
         qbs = {}
 
-        def mx(j):
-            pb = psum.tile([P, 512], F32, name="pb")
+        def pass_d1_d3(j):
+            pb = psum.tile([P, 512], F32, name="pb", tag="for_scalar")
             pbs[j] = pb
             for s in range(2):
-                col = ((2 * j + s) % 4) * P
-                nc.tensor.matmul_mx(
-                    out=pb[:, s * 256 : (s + 1) * 256],
-                    lhsT=x_codes[j // 2][:, col : col + P].bitcast(FP8X4),
-                    lhsT_scale=x_scales[j // 2][:, col : col + P],
-                    rhs=up_codes[:].bitcast(FP8X4),
-                    rhs_scale=up_scales[:],
-                    start=True,
-                    stop=True,
-                )
-            for s in range(2):
-                col = ((2 * j + s) % 4) * P
-                qb = psum.tile([P, 512], F32, name="qb", bufs=4)
-                qbs[2 * j + s] = qb
-                nc.tensor.matmul_mx(
-                    out=qb[:],
-                    lhsT=x_codes[j // 2][:, col : col + P].bitcast(FP8X4),
-                    lhsT_scale=x_scales[j // 2][:, col : col + P],
-                    rhs=uq_codes[:].bitcast(FP8X4),
-                    rhs_scale=uq_scales[:],
-                    start=True,
-                    stop=True,
-                )
+                mx(pb[:, s * 256 : (s + 1) * 256], 2 * j + s, up_codes[:], up_scales[:])
 
-        a3s = {}
+        def pass_d0(g):
+            tiles = [t for t in range(4 * g, 4 * g + 4) if d0_on_scalar(t)]
+            db = psum.tile([P, 512], F32, name="db", tag="for_scalar")
+            dbs[g] = db
+            for i, t in enumerate(tiles):
+                mx(db[:, i * R : (i + 1) * R], t, uq_codes[:, 0:R], uq_scales[:, 0:R])
+
+        def pass_rest(t):
+            qb = psum.tile([P, 512], F32, name="qb", tag="for_vector")
+            qbs[t] = qb
+            if d0_on_scalar(t):
+                mx(qb[:, 128:384], t, uq_codes[:, 128:384], uq_scales[:, 128:384])
+                mx(qb[:, 384:512], t, uq_codes[:, 384:512], uq_scales[:, 384:512])
+            else:
+                mx(qb[:], t, uq_codes[:], uq_scales[:])
 
         def copies(j):
             pb = pbs[j][:].rearrange("p (s c) -> p s c", s=2)
-            a3 = work.tile([P, 2, R], F32, name="a3")
-            a3s[j] = a3
-            nc.scalar.copy(out=a3[:], in_=pb[:, :, 128:256])
+            nc.scalar.copy(out=a3s[j % FIN_BUFS][:], in_=pb[:, :, 128:256])
             nc.scalar.activation(
-                out=fins[j % FIN_BUFS][:, :, 0, :], in_=pb[:, :, 0:128], func=COPY, scale=c_f[:, 1:2]
+                out=fins[j % FIN_BUFS][:, :, 1, :], in_=pb[:, :, 0:128], func=COPY, scale=c_f[:, 1:2]
             )
 
-        def linear_sums(j):
-            for t in (2 * j, 2 * j + 1):
-                if d0_on_scalar(t):
-                    junk_s = work.tile([P, R], F32, name="junk_s", bufs=4)
-                    nc.scalar.activation(
-                        out=junk_s[:], in_=qbs[t][:, 256:384], func=COPY, accum_out=s0[:, t : t + 1]
-                    )
-
-        def vector_part(j):
-            fin = fins[j % FIN_BUFS]
-            for s in range(2):
-                nc.vector.scalar_tensor_tensor(
-                    out=fin[:, s, 2, :],
-                    in0=a3s[j][:, s, :],
-                    scalar=c_f[:, 2:3],
-                    in1=qbs[2 * j + s][:, 0:128],
-                    op0=MULT,
-                    op1=MULT,
+        def linear_sums(g):
+            tiles = [t for t in range(4 * g, 4 * g + 4) if d0_on_scalar(t)]
+            for i, t in enumerate(tiles):
+                junk_s = work.tile([P, R], F32, name="junk_s")
+                nc.scalar.activation(
+                    out=junk_s[:],
+                    in_=dbs[g][:, i * R : (i + 1) * R],
+                    func=COPY,
+                    accum_out=s0[:, t : t + 1],
                 )
-            for s in range(2):
-                t = 2 * j + s
-                if t == TILES - 1:
+
+        def cubic_head(t):
+            nc.vector.scalar_tensor_tensor(
+                out=fins[(t // 2) % FIN_BUFS][:, t % 2, 2, :],
+                in0=a3s[(t // 2) % FIN_BUFS][:, t % 2, :],
+                scalar=c_f[:, 2:3],
+                in1=qbs[t][:, 384:512],
+                op0=MULT,
+                op1=MULT,
+            )
+
+        def sums(t):
+            fin = fins[(t // 2) % FIN_BUFS]
+            junk_v = work.tile([P, 3 * R], F32, name="junk_v")
+            lo = 1 if d0_on_scalar(t) else 0
+            nc.vector.scalar_tensor_tensor(
+                out=junk_v[:, lo * R : 3 * R],
+                in0=fin[:, t % 2, lo:3, :].rearrange("p b r -> p (b r)"),
+                scalar=1.0,
+                in1=qbs[t][:, lo * R : 3 * R],
+                op0=MULT,
+                op1=MULT,
+                accum_out=acc[:, t : t + 1],
+            )
+
+        regroup_u(0)
+        regroup_u(1)
+        quantise_u(0)
+        constants()
+        regroup_u(2)
+        regroup_u(3)
+        quantise_u(2)
+        regroup_u(4)
+        regroup_u(5)
+        quantise_u(4)
+
+        for r in range(-X_LEAD, ROUNDS):
+            gx, gq, gs = r + X_LEAD, r + Q_LEAD, r + S_LEAD
+            if gx < ROUNDS:
+                transposes(2 * gx)
+                transposes(2 * gx + 1)
+                copy_xt(2 * gx)
+                copy_xt(2 * gx + 1)
+            side = 0 <= gs < ROUNDS
+            if r >= 0:
+                pass_rest(4 * r)
+            if side:
+                pass_d1_d3(2 * gs)
+            if r >= 0:
+                pass_rest(4 * r + 1)
+            if side:
+                pass_d1_d3(2 * gs + 1)
+            if r >= 0:
+                pass_rest(4 * r + 2)
+            if side:
+                pass_d0(gs)
+            if r >= 0:
+                pass_rest(4 * r + 3)
+            if side:
+                copies(2 * gs)
+                copies(2 * gs + 1)
+                linear_sums(gs)
+            if r >= 0:
+                cubic_head(4 * r)
+            if 0 <= gq < ROUNDS:
+                quantise_x(gq)
+            if r >= 0:
+                cubic_head(4 * r + 1)
+                sums(4 * r)
+                cubic_head(4 * r + 2)
+                sums(4 * r + 1)
+                cubic_head(4 * r + 3)
+                sums(4 * r + 2)
+                if r == ROUNDS - 1:
                     nc.vector.tensor_scalar(
                         out=part[:],
                         in0=s0[:],
@@ -248,69 +310,7 @@ def tile_polynomialtensorregression_pa_t_kernel(
                         op0=MULT,
                         op1=ADD,
                     )
-                junk_v = work.tile([P, 3, R], F32, name="junk_v", bufs=4)
-                rest = qbs[t][:, 128:512].rearrange("p (b r) -> p b r", b=3)
-                if d0_on_scalar(t):
-                    nc.vector.scalar_tensor_tensor(
-                        out=junk_v[:, 0:2, :],
-                        in0=fin[:, s, 0:3:2, :],
-                        scalar=1.0,
-                        in1=rest[:, 0:3:2, :],
-                        op0=MULT,
-                        op1=MULT,
-                        accum_out=acc[:, t : t + 1],
-                    )
-                else:
-                    nc.vector.scalar_tensor_tensor(
-                        out=junk_v[:],
-                        in0=fin[:, s, :, :],
-                        scalar=1.0,
-                        in1=rest,
-                        op0=MULT,
-                        op1=MULT,
-                        accum_out=acc[:, t : t + 1],
-                    )
-
-        transposes(0)
-        copy_xt(0)
-        regroup_u(0)
-        regroup_u(1)
-        quantise_u(0)
-        constants()
-        quantise_x(0, 1)
-        transposes(1)
-        copy_xt(1)
-        regroup_u(2)
-        regroup_u(3)
-        quantise_u(2)
-        quantise_x(1, 1)
-        regroup_u(4)
-        regroup_u(5)
-        quantise_u(4)
-
-        done = {"transposed": 2, "copied": 2, "quantised": 2}
-
-        def copy_one():
-            if done["copied"] < done["transposed"]:
-                copy_xt(done["copied"])
-                done["copied"] += 1
-
-        for j in range(PAIRS):
-            copy_one()
-            mx(j)
-            copies(j)
-            copy_one()
-            linear_sums(j)
-            vector_part(j)
-            if done["quantised"] + 2 <= done["copied"]:
-                quantise_x(done["quantised"], 2)
-                done["quantised"] += 2
-            if (j < RAMP or j % 2 == 1) and done["transposed"] < PAIRS:
-                copy_one()
-                copy_one()
-                transposes(done["transposed"])
-                transposes(done["transposed"] + 1)
-                done["transposed"] += 2
+                sums(4 * r + 3)
 
         nc.vector.tensor_tensor(out=res[:], in0=part[:], in1=acc[:], op=ADD)
         nc.sync.dma_start(out=out.rearrange("(p t) -> p t", t=TILES), in_=res[:])

@@ -19,14 +19,14 @@ PAIRS = TILES // 2
 ROUNDS = TILES // 4
 FLOPS = 2 * B * D * R * 6
 CHUNKS = (2, 2, 4, 4, 4, 8, 8, 8, 8, 8, 8)
-X_LEAD = 3
+X_LEAD = 2
 Q_LEAD = 2
 S_LEAD = 1
 FIN_BUFS = 6
 
 
 def d0_on_scalar(t):
-    return t >= 48 or t % 4 != 3
+    return t >= 4 and (t >= 48 or t % 4 != 3)
 
 
 def tile_polynomialtensorregression_pa_t_kernel(
@@ -132,6 +132,8 @@ def tile_polynomialtensorregression_pa_t_kernel(
         def constants():
             nc.vector.tensor_copy(out=c_f[:], in_=c_bf[:])
             nc.vector.tensor_copy(out=b_f[:], in_=b_bf[:])
+
+        def fill_c0():
             for fin in fins:
                 nc.vector.tensor_scalar(
                     out=fin[:, :, 0, :],
@@ -197,10 +199,11 @@ def tile_polynomialtensorregression_pa_t_kernel(
 
         def pass_d0(g):
             tiles = [t for t in range(4 * g, 4 * g + 4) if d0_on_scalar(t)]
-            db = psum.tile([P, 512], F32, name="db", tag="for_scalar")
-            dbs[g] = db
+            if tiles:
+                db = psum.tile([P, 512], F32, name="db", tag="for_scalar")
+                dbs[g] = db
             for i, t in enumerate(tiles):
-                mx(db[:, i * R : (i + 1) * R], t, uq_codes[:, 0:R], uq_scales[:, 0:R])
+                mx(dbs[g][:, i * R : (i + 1) * R], t, uq_codes[:, 0:R], uq_scales[:, 0:R])
 
         def pass_rest(t):
             qb = psum.tile([P, 512], F32, name="qb", tag="for_vector")
@@ -256,13 +259,13 @@ def tile_polynomialtensorregression_pa_t_kernel(
         regroup_u(0)
         regroup_u(1)
         quantise_u(0)
-        constants()
         regroup_u(2)
         regroup_u(3)
         quantise_u(2)
         regroup_u(4)
         regroup_u(5)
         quantise_u(4)
+        constants()
 
         for r in range(-X_LEAD, ROUNDS):
             gx, gq, gs = r + X_LEAD, r + Q_LEAD, r + S_LEAD
@@ -292,12 +295,14 @@ def tile_polynomialtensorregression_pa_t_kernel(
                 linear_sums(gs)
             if r >= 0:
                 cubic_head(4 * r)
-            if 0 <= gq < ROUNDS:
-                quantise_x(gq)
-            if r >= 0:
                 cubic_head(4 * r + 1)
                 sums(4 * r)
                 cubic_head(4 * r + 2)
+            if 0 <= gq < ROUNDS:
+                quantise_x(gq)
+            if gq == 0:
+                fill_c0()
+            if r >= 0:
                 sums(4 * r + 1)
                 cubic_head(4 * r + 3)
                 sums(4 * r + 2)

@@ -19,14 +19,14 @@ PAIRS = TILES // 2
 ROUNDS = TILES // 4
 FLOPS = 2 * B * D * R * 6
 CHUNKS = (2, 2, 4, 4, 4, 8, 8, 8, 8, 8, 8)
-X_LEAD = 2
+X_LEAD = 3
 Q_LEAD = 2
 S_LEAD = 1
 FIN_BUFS = 6
 
 
 def d0_on_scalar(t):
-    return t >= 4 and (t >= 48 or t % 4 != 3)
+    return t >= 48 or t % 4 != 3
 
 
 def tile_polynomialtensorregression_pa_t_kernel(
@@ -39,17 +39,17 @@ def tile_polynomialtensorregression_pa_t_kernel(
         psum = ctx.enter_context(tc.psum_pool(name="psum", bufs=4))
         ctx.enter_context(tc.manual_schedule())
 
+        c_bf = keep.tile([P, 3], BF16, name="c_bf")
+        b_bf = keep.tile([P, 1], BF16, name="b_bf")
+        nc.scalar.dma_start(out=c_bf[:], in_=C.partition_broadcast(P))
+        nc.scalar.dma_start(out=b_bf[:], in_=beta.partition_broadcast(P))
+
         ident = keep.tile([P, P], F32, name="ident")
         make_identity(nc, ident[:])
         warm = keep.tile([P, 1], F32, name="warm")
         warm2 = keep.tile([P, 1], F32, name="warm2")
         nc.vector.memset(warm[:], 0.0)
         nc.scalar.activation(out=warm2[:], in_=warm[:], func=COPY)
-
-        c_bf = keep.tile([P, 3], BF16, name="c_bf")
-        b_bf = keep.tile([P, 1], BF16, name="b_bf")
-        nc.scalar.dma_start(out=c_bf[:], in_=C.partition_broadcast(P))
-        nc.scalar.dma_start(out=b_bf[:], in_=beta.partition_broadcast(P))
 
         x_view = X.rearrange("(p t) k -> p t k", t=TILES)
         x_of = []
@@ -199,11 +199,10 @@ def tile_polynomialtensorregression_pa_t_kernel(
 
         def pass_d0(g):
             tiles = [t for t in range(4 * g, 4 * g + 4) if d0_on_scalar(t)]
-            if tiles:
-                db = psum.tile([P, 512], F32, name="db", tag="for_scalar")
-                dbs[g] = db
+            db = psum.tile([P, 512], F32, name="db", tag="for_scalar")
+            dbs[g] = db
             for i, t in enumerate(tiles):
-                mx(dbs[g][:, i * R : (i + 1) * R], t, uq_codes[:, 0:R], uq_scales[:, 0:R])
+                mx(db[:, i * R : (i + 1) * R], t, uq_codes[:, 0:R], uq_scales[:, 0:R])
 
         def pass_rest(t):
             qb = psum.tile([P, 512], F32, name="qb", tag="for_vector")
@@ -265,7 +264,6 @@ def tile_polynomialtensorregression_pa_t_kernel(
         regroup_u(4)
         regroup_u(5)
         quantise_u(4)
-        constants()
 
         for r in range(-X_LEAD, ROUNDS):
             gx, gq, gs = r + X_LEAD, r + Q_LEAD, r + S_LEAD
@@ -295,14 +293,16 @@ def tile_polynomialtensorregression_pa_t_kernel(
                 linear_sums(gs)
             if r >= 0:
                 cubic_head(4 * r)
-                cubic_head(4 * r + 1)
-                sums(4 * r)
-                cubic_head(4 * r + 2)
             if 0 <= gq < ROUNDS:
                 quantise_x(gq)
             if gq == 0:
+                constants()
+            if gq == 1:
                 fill_c0()
             if r >= 0:
+                cubic_head(4 * r + 1)
+                sums(4 * r)
+                cubic_head(4 * r + 2)
                 sums(4 * r + 1)
                 cubic_head(4 * r + 3)
                 sums(4 * r + 2)

@@ -19,14 +19,14 @@ PAIRS = TILES // 2
 ROUNDS = TILES // 4
 FLOPS = 2 * B * D * R * 6
 CHUNKS = (2, 2, 4, 4, 4, 8, 8, 8, 8, 8, 8)
-X_LEAD = 3
+X_LEAD = 2
 Q_LEAD = 2
 S_LEAD = 1
-FIN_BUFS = 6
+FIN_BUFS = 3
 
 
-def d0_on_scalar(t):
-    return t >= 48 or t % 4 != 3
+def d0_on_vector(g):
+    return g < 12 and g % 3 == 0
 
 
 def tile_polynomialtensorregression_pa_t_kernel(
@@ -81,9 +81,10 @@ def tile_polynomialtensorregression_pa_t_kernel(
         load_u(0)
         load_u(1)
         load_x(1)
+        load_x(2)
         for i in range(2, 6):
             load_u(i)
-        for c in range(2, len(CHUNKS)):
+        for c in range(3, len(CHUNKS)):
             load_x(c)
 
         u_grp = []
@@ -107,11 +108,8 @@ def tile_polynomialtensorregression_pa_t_kernel(
         fins = []
         a3s = []
         for n in range(FIN_BUFS):
-            fin = keep.tile([P, 2, 3, R], F32, name="fin%d" % n)
-            fins.append(fin)
-            nc.vector.memset(fin[:, :, 0, :], 1.0)
-            a3s.append(keep.tile([P, 2, R], F32, name="a3_%d" % n))
-        nc.vector.memset(s0[:], 0.0)
+            fins.append(keep.tile([P, 4, 2, R], F32, name="fin%d" % n))
+            a3s.append(keep.tile([P, 4, R], F32, name="a3_%d" % n))
 
         def regroup_u(i):
             nc.vector.tensor_copy(
@@ -132,16 +130,6 @@ def tile_polynomialtensorregression_pa_t_kernel(
         def constants():
             nc.vector.tensor_copy(out=c_f[:], in_=c_bf[:])
             nc.vector.tensor_copy(out=b_f[:], in_=b_bf[:])
-
-        def fill_c0():
-            for fin in fins:
-                nc.vector.tensor_scalar(
-                    out=fin[:, :, 0, :],
-                    in0=fin[:, :, 0, :],
-                    scalar1=c_f[:, 0:1],
-                    scalar2=None,
-                    op0=MULT,
-                )
 
         def mx(bank, t, codes, scales):
             col = (t % 4) * P
@@ -190,6 +178,7 @@ def tile_polynomialtensorregression_pa_t_kernel(
         pbs = {}
         dbs = {}
         qbs = {}
+        q4s = {}
 
         def pass_d1_d3(j):
             pb = psum.tile([P, 512], F32, name="pb", tag="for_scalar")
@@ -198,58 +187,69 @@ def tile_polynomialtensorregression_pa_t_kernel(
                 mx(pb[:, s * 256 : (s + 1) * 256], 2 * j + s, up_codes[:], up_scales[:])
 
         def pass_d0(g):
-            tiles = [t for t in range(4 * g, 4 * g + 4) if d0_on_scalar(t)]
-            db = psum.tile([P, 512], F32, name="db", tag="for_scalar")
+            side = "for_vector" if d0_on_vector(g) else "for_scalar"
+            db = psum.tile([P, 512], F32, name="db", tag=side)
             dbs[g] = db
-            for i, t in enumerate(tiles):
-                mx(db[:, i * R : (i + 1) * R], t, uq_codes[:, 0:R], uq_scales[:, 0:R])
+            for i in range(4):
+                mx(db[:, i * R : (i + 1) * R], 4 * g + i, uq_codes[:, 0:R], uq_scales[:, 0:R])
 
-        def pass_rest(t):
+        def pass_d4(g):
+            q4 = psum.tile([P, 512], F32, name="q4", tag="for_vector")
+            q4s[g] = q4
+            for i in range(4):
+                mx(q4[:, i * R : (i + 1) * R], 4 * g + i, uq_codes[:, 384:512], uq_scales[:, 384:512])
+
+        def pass_d2_d5(j):
             qb = psum.tile([P, 512], F32, name="qb", tag="for_vector")
-            qbs[t] = qb
-            if d0_on_scalar(t):
-                mx(qb[:, 128:384], t, uq_codes[:, 128:384], uq_scales[:, 128:384])
-                mx(qb[:, 384:512], t, uq_codes[:, 384:512], uq_scales[:, 384:512])
-            else:
-                mx(qb[:], t, uq_codes[:], uq_scales[:])
+            qbs[j] = qb
+            for s in range(2):
+                mx(qb[:, s * 256 : (s + 1) * 256], 2 * j + s, uq_codes[:, 128:384], uq_scales[:, 128:384])
 
         def copies(j):
             pb = pbs[j][:].rearrange("p (s c) -> p s c", s=2)
-            nc.scalar.copy(out=a3s[j % FIN_BUFS][:], in_=pb[:, :, 128:256])
+            n = (j // 2) % FIN_BUFS
+            lo = 2 * (j % 2)
+            nc.scalar.copy(out=a3s[n][:, lo : lo + 2, :], in_=pb[:, :, 128:256])
             nc.scalar.activation(
-                out=fins[j % FIN_BUFS][:, :, 1, :], in_=pb[:, :, 0:128], func=COPY, scale=c_f[:, 1:2]
+                out=fins[n][:, lo : lo + 2, 0, :], in_=pb[:, :, 0:128], func=COPY, scale=c_f[:, 1:2]
             )
 
         def linear_sums(g):
-            tiles = [t for t in range(4 * g, 4 * g + 4) if d0_on_scalar(t)]
-            for i, t in enumerate(tiles):
+            if d0_on_vector(g):
+                nc.vector.tensor_reduce(
+                    out=s0[:, 4 * g : 4 * g + 4],
+                    in_=dbs[g][:].rearrange("p (s r) -> p s r", s=4),
+                    op=ADD,
+                    axis=mybir.AxisListType.X,
+                )
+                return
+            for i in range(4):
                 junk_s = work.tile([P, R], F32, name="junk_s")
                 nc.scalar.activation(
                     out=junk_s[:],
                     in_=dbs[g][:, i * R : (i + 1) * R],
                     func=COPY,
-                    accum_out=s0[:, t : t + 1],
+                    accum_out=s0[:, 4 * g + i : 4 * g + i + 1],
                 )
 
-        def cubic_head(t):
+        def cubic_head(g):
             nc.vector.scalar_tensor_tensor(
-                out=fins[(t // 2) % FIN_BUFS][:, t % 2, 2, :],
-                in0=a3s[(t // 2) % FIN_BUFS][:, t % 2, :],
+                out=fins[g % FIN_BUFS][:, :, 1, :],
+                in0=a3s[g % FIN_BUFS][:],
                 scalar=c_f[:, 2:3],
-                in1=qbs[t][:, 384:512],
+                in1=q4s[g][:].rearrange("p (s r) -> p s r", s=4),
                 op0=MULT,
                 op1=MULT,
             )
 
         def sums(t):
-            fin = fins[(t // 2) % FIN_BUFS]
-            junk_v = work.tile([P, 3 * R], F32, name="junk_v")
-            lo = 1 if d0_on_scalar(t) else 0
+            fin = fins[(t // 4) % FIN_BUFS]
+            junk_v = work.tile([P, 2 * R], F32, name="junk_v")
             nc.vector.scalar_tensor_tensor(
-                out=junk_v[:, lo * R : 3 * R],
-                in0=fin[:, t % 2, lo:3, :].rearrange("p b r -> p (b r)"),
+                out=junk_v[:],
+                in0=fin[:, t % 4, :, :].rearrange("p b r -> p (b r)"),
                 scalar=1.0,
-                in1=qbs[t][:, lo * R : 3 * R],
+                in1=qbs[t // 2][:, (t % 2) * 256 : (t % 2 + 1) * 256],
                 op0=MULT,
                 op1=MULT,
                 accum_out=acc[:, t : t + 1],
@@ -258,12 +258,6 @@ def tile_polynomialtensorregression_pa_t_kernel(
         regroup_u(0)
         regroup_u(1)
         quantise_u(0)
-        regroup_u(2)
-        regroup_u(3)
-        quantise_u(2)
-        regroup_u(4)
-        regroup_u(5)
-        quantise_u(4)
 
         for r in range(-X_LEAD, ROUNDS):
             gx, gq, gs = r + X_LEAD, r + Q_LEAD, r + S_LEAD
@@ -274,47 +268,47 @@ def tile_polynomialtensorregression_pa_t_kernel(
                 copy_xt(2 * gx + 1)
             side = 0 <= gs < ROUNDS
             if r >= 0:
-                pass_rest(4 * r)
+                pass_d4(r)
             if side:
                 pass_d1_d3(2 * gs)
             if r >= 0:
-                pass_rest(4 * r + 1)
+                pass_d2_d5(2 * r)
             if side:
                 pass_d1_d3(2 * gs + 1)
             if r >= 0:
-                pass_rest(4 * r + 2)
+                pass_d2_d5(2 * r + 1)
             if side:
                 pass_d0(gs)
-            if r >= 0:
-                pass_rest(4 * r + 3)
-            if side:
                 copies(2 * gs)
                 copies(2 * gs + 1)
-                linear_sums(gs)
             if r >= 0:
-                cubic_head(4 * r)
+                cubic_head(r)
             if 0 <= gq < ROUNDS:
                 quantise_x(gq)
             if gq == 0:
                 constants()
-            if gq == 1:
-                fill_c0()
+                regroup_u(2)
+                regroup_u(3)
+                quantise_u(2)
+                regroup_u(4)
+                regroup_u(5)
+                quantise_u(4)
             if r >= 0:
-                cubic_head(4 * r + 1)
                 sums(4 * r)
-                cubic_head(4 * r + 2)
                 sums(4 * r + 1)
-                cubic_head(4 * r + 3)
                 sums(4 * r + 2)
-                if r == ROUNDS - 1:
-                    nc.vector.tensor_scalar(
-                        out=part[:],
-                        in0=s0[:],
-                        scalar1=c_f[:, 0:1],
-                        scalar2=b_f[:, 0:1],
-                        op0=MULT,
-                        op1=ADD,
-                    )
+            if side:
+                linear_sums(gs)
+            if r == ROUNDS - 1:
+                nc.vector.tensor_scalar(
+                    out=part[:],
+                    in0=s0[:],
+                    scalar1=c_f[:, 0:1],
+                    scalar2=b_f[:, 0:1],
+                    op0=MULT,
+                    op1=ADD,
+                )
+            if r >= 0:
                 sums(4 * r + 3)
 
         nc.vector.tensor_tensor(out=res[:], in0=part[:], in1=acc[:], op=ADD)

@@ -25,8 +25,12 @@ S_LEAD = 1
 FIN_BUFS = 3
 
 
+LATE_FROM = 8
+LATE_TURNS = {13: (8, 9, 10), 14: (11, 12, 13), 15: (14, 15)}
+
+
 def d0_on_vector(g):
-    return g < 12 and g % 3 == 0
+    return g in (0, 2, 5)
 
 
 def tile_polynomialtensorregression_pa_t_kernel(
@@ -277,10 +281,15 @@ def tile_polynomialtensorregression_pa_t_kernel(
                 pass_d1_d3(2 * gs + 1)
             if r >= 0:
                 pass_d2_d5(2 * r + 1)
-            if side:
+            linear = side and gs < LATE_FROM
+            if linear:
                 pass_d0(gs)
+            if side:
                 copies(2 * gs)
                 copies(2 * gs + 1)
+            for g in LATE_TURNS.get(r, ()):
+                pass_d0(g)
+                linear_sums(g)
             if r >= 0:
                 cubic_head(r)
             if 0 <= gq < ROUNDS:
@@ -297,7 +306,7 @@ def tile_polynomialtensorregression_pa_t_kernel(
                 sums(4 * r)
                 sums(4 * r + 1)
                 sums(4 * r + 2)
-            if side:
+            if linear:
                 linear_sums(gs)
             if r == ROUNDS - 1:
                 nc.vector.tensor_scalar(

@@ -43,10 +43,12 @@ def tile_polynomialtensorregression_pa_t_kernel(
         psum = ctx.enter_context(tc.psum_pool(name="psum", bufs=4))
         ctx.enter_context(tc.manual_schedule())
 
-        c_bf = keep.tile([P, 3], BF16, name="c_bf")
-        b_bf = keep.tile([P, 1], BF16, name="b_bf")
-        nc.scalar.dma_start(out=c_bf[:], in_=C.partition_broadcast(P))
-        nc.scalar.dma_start(out=b_bf[:], in_=beta.partition_broadcast(P))
+        cb_row = keep.tile([P, 32], BF16, name="cb_row")
+        nc.gpsimd.memset(cb_row[:], 0.0)
+        nc.scalar.dma_start(out=cb_row[0:1, 0:3], in_=C.rearrange("(o c) -> o c", o=1))
+        nc.scalar.dma_start(out=cb_row[0:1, 16:17], in_=beta.rearrange("(o c) -> o c", o=1))
+        ones = keep.tile([P, P], BF16, name="ones")
+        nc.vector.memset(ones[:], 1.0)
 
         ident = keep.tile([P, P], F32, name="ident")
         make_identity(nc, ident[:])
@@ -103,8 +105,7 @@ def tile_polynomialtensorregression_pa_t_kernel(
         for g in range(ROUNDS):
             x_codes.append(keep.tile([P, 4 * P], U32, name="x_codes%d" % g, align_bytes=64))
             x_scales.append(keep.tile([P, 4 * P], U8, name="x_scales%d" % g, align_bytes=64))
-        c_f = keep.tile([P, 3], F32, name="c_f")
-        b_f = keep.tile([P, 1], F32, name="b_f")
+        cb_f = keep.tile([P, 32], F32, name="cb_f")
         s0 = keep.tile([P, TILES], F32, name="s0")
         acc = keep.tile([P, TILES], F32, name="acc")
         part = keep.tile([P, TILES], F32, name="part")
@@ -131,9 +132,13 @@ def tile_polynomialtensorregression_pa_t_kernel(
                 scales = uq_scales[:, (i - 2) * R : i * R]
             nc.vector.quantize_mx(out=codes.bitcast(FP8X4), scales=scales, in_=u_grp[i // 2][:])
 
-        def constants():
-            nc.vector.tensor_copy(out=c_f[:], in_=c_bf[:])
-            nc.vector.tensor_copy(out=b_f[:], in_=b_bf[:])
+        def spread_constants():
+            spread = psum.tile([P, 512], F32, name="spread", tag="for_vector")
+            nc.tensor.matmul(out=spread[:, 0:32], lhsT=ones[:], rhs=cb_row[:], start=True, stop=True)
+            return spread
+
+        def constants(spread):
+            nc.vector.tensor_copy(out=cb_f[:], in_=spread[:, 0:32])
 
         def mx(bank, t, codes, scales):
             col = (t % 4) * P
@@ -215,7 +220,7 @@ def tile_polynomialtensorregression_pa_t_kernel(
             lo = 2 * (j % 2)
             nc.scalar.copy(out=a3s[n][:, lo : lo + 2, :], in_=pb[:, :, 128:256])
             nc.scalar.activation(
-                out=fins[n][:, lo : lo + 2, 0, :], in_=pb[:, :, 0:128], func=COPY, scale=c_f[:, 1:2]
+                out=fins[n][:, lo : lo + 2, 0, :], in_=pb[:, :, 0:128], func=COPY, scale=cb_f[:, 1:2]
             )
 
         def linear_sums(g):
@@ -240,7 +245,7 @@ def tile_polynomialtensorregression_pa_t_kernel(
             nc.vector.scalar_tensor_tensor(
                 out=fins[g % FIN_BUFS][:, :, 1, :],
                 in0=a3s[g % FIN_BUFS][:],
-                scalar=c_f[:, 2:3],
+                scalar=cb_f[:, 2:3],
                 in1=q4s[g][:].rearrange("p (s r) -> p s r", s=4),
                 op0=MULT,
                 op1=MULT,
@@ -270,6 +275,8 @@ def tile_polynomialtensorregression_pa_t_kernel(
                 transposes(2 * gx + 1)
                 copy_xt(2 * gx)
                 copy_xt(2 * gx + 1)
+            if gq == 0:
+                spread = spread_constants()
             side = 0 <= gs < ROUNDS
             if r >= 0:
                 pass_d4(r)
@@ -295,7 +302,7 @@ def tile_polynomialtensorregression_pa_t_kernel(
             if 0 <= gq < ROUNDS:
                 quantise_x(gq)
             if gq == 0:
-                constants()
+                constants(spread)
                 regroup_u(2)
                 regroup_u(3)
                 quantise_u(2)
@@ -312,8 +319,8 @@ def tile_polynomialtensorregression_pa_t_kernel(
                 nc.vector.tensor_scalar(
                     out=part[:],
                     in0=s0[:],
-                    scalar1=c_f[:, 0:1],
-                    scalar2=b_f[:, 0:1],
+                    scalar1=cb_f[:, 0:1],
+                    scalar2=cb_f[:, 16:17],
                     op0=MULT,
                     op1=ADD,
                 )

@@ -45,8 +45,6 @@ def tile_polynomialtensorregression_pa_t_kernel(
 
         cb_row = keep.tile([P, 32], BF16, name="cb_row")
         nc.gpsimd.memset(cb_row[:], 0.0)
-        nc.scalar.dma_start(out=cb_row[0:1, 0:3], in_=C.rearrange("(o c) -> o c", o=1))
-        nc.scalar.dma_start(out=cb_row[0:1, 16:17], in_=beta.rearrange("(o c) -> o c", o=1))
         ones = keep.tile([P, P], BF16, name="ones")
         nc.vector.memset(ones[:], 1.0)
 
@@ -56,6 +54,8 @@ def tile_polynomialtensorregression_pa_t_kernel(
         warm2 = keep.tile([P, 1], F32, name="warm2")
         nc.vector.memset(warm[:], 0.0)
         nc.scalar.activation(out=warm2[:], in_=warm[:], func=COPY)
+        nc.scalar.dma_start(out=cb_row[0:1, 0:3], in_=C.rearrange("(o c) -> o c", o=1))
+        nc.scalar.dma_start(out=cb_row[0:1, 16:17], in_=beta.rearrange("(o c) -> o c", o=1))
 
         x_view = X.rearrange("(p t) k -> p t k", t=TILES)
         x_of = []
@@ -275,8 +275,12 @@ def tile_polynomialtensorregression_pa_t_kernel(
                 transposes(2 * gx + 1)
                 copy_xt(2 * gx)
                 copy_xt(2 * gx + 1)
-            if gq == 0:
+            if gq == 1:
                 spread = spread_constants()
+                constants(spread)
+                regroup_u(4)
+                regroup_u(5)
+                quantise_u(4)
             side = 0 <= gs < ROUNDS
             if r >= 0:
                 pass_d4(r)
@@ -302,13 +306,9 @@ def tile_polynomialtensorregression_pa_t_kernel(
             if 0 <= gq < ROUNDS:
                 quantise_x(gq)
             if gq == 0:
-                constants(spread)
                 regroup_u(2)
                 regroup_u(3)
                 quantise_u(2)
-                regroup_u(4)
-                regroup_u(5)
-                quantise_u(4)
             if r >= 0:
                 sums(4 * r)
                 sums(4 * r + 1)

from contextlib import ExitStack

import concourse.mybir as mybir
from concourse.masks import make_identity

FP8X4 = mybir.dt.float8_e4m3fn_x4
BF16 = mybir.dt.bfloat16
F32 = mybir.dt.float32
U32 = mybir.dt.uint32
U8 = mybir.dt.uint8
MULT = mybir.AluOpType.mult
ADD = mybir.AluOpType.add
COPY = mybir.ActivationFunctionType.Copy

B, D, R = 8192, 512, 128
P = 128
TILES = B // P
PAIRS = TILES // 2
ROUNDS = TILES // 4
FLOPS = 2 * B * D * R * 6
CHUNKS = (2, 2, 4, 4, 4, 8, 8, 8, 8, 8, 8)
X_LEAD = 2
Q_LEAD = 2
S_LEAD = 1
FIN_BUFS = 3


LATE_FROM = 8
LATE_TURNS = {13: (8, 9, 10), 14: (11, 12, 13), 15: (14, 15)}


def d0_on_vector(g):
    return g in (0, 2, 5)


def tile_polynomialtensorregression_pa_t_kernel(
    tc, X, U_0_0, U_1_0, U_1_1, U_2_0, U_2_1, U_2_2, C, beta, out
):
    nc = tc.nc
    with ExitStack() as ctx:
        keep = ctx.enter_context(tc.tile_pool(name="keep", bufs=1))
        work = ctx.enter_context(tc.tile_pool(name="work", bufs=4))
        psum = ctx.enter_context(tc.psum_pool(name="psum", bufs=4))
        ctx.enter_context(tc.manual_schedule())

        cb_row = keep.tile([P, 32], BF16, name="cb_row")
        nc.gpsimd.memset(cb_row[:], 0.0)
        ones = keep.tile([P, P], BF16, name="ones")
        nc.vector.memset(ones[:], 1.0)

        ident = keep.tile([P, P], F32, name="ident")
        make_identity(nc, ident[:])
        warm = keep.tile([P, 1], F32, name="warm")
        warm2 = keep.tile([P, 1], F32, name="warm2")
        nc.vector.memset(warm[:], 0.0)
        nc.scalar.activation(out=warm2[:], in_=warm[:], func=COPY)
        nc.scalar.dma_start(out=cb_row[0:1, 0:3], in_=C.rearrange("(o c) -> o c", o=1))
        nc.scalar.dma_start(out=cb_row[0:1, 16:17], in_=beta.rearrange("(o c) -> o c", o=1))

        x_view = X.rearrange("(p t) k -> p t k", t=TILES)
        x_of = []
        x_chunks = []
        first = 0
        for c, n in enumerate(CHUNKS):
            x_sb = keep.tile([P, n, D], BF16, name="x%d" % c)
            x_chunks.append((x_sb, first, n))
            for i in range(n):
                x_of.append((x_sb, i))
            first += n

        def load_x(c):
            x_sb, t0, n = x_chunks[c]
            nc.sync.dma_start(out=x_sb[:], in_=x_view[:, t0 : t0 + n, :])

        u_order = (U_1_0, U_2_0, U_0_0, U_1_1, U_2_2, U_2_1)
        u_raw = []

        def load_u(i):
            raw = keep.tile([P, D], BF16, name="u_raw%d" % i)
            u_raw.append(raw)
            nc.sync.dma_start(
                out=raw[:].rearrange("p (u e c) -> p u e c", u=2, e=2),
                in_=u_order[i].rearrange("(u q e) c -> q u e c", u=2, e=2),
            )

        load_x(0)
        load_u(0)
        load_u(1)
        load_x(1)
        load_x(2)
        for i in range(2, 6):
            load_u(i)
        for c in range(3, len(CHUNKS)):
            load_x(c)

        u_grp = []
        for n in range(3):
            u_grp.append(keep.tile([P, 2 * D], BF16, name="u_grp%d" % n, align_bytes=64))
        up_codes = keep.tile([P, 2 * R], U32, name="up_codes", align_bytes=64)
        up_scales = keep.tile([P, 2 * R], U8, name="up_scales", align_bytes=64)
        uq_codes = keep.tile([P, 4 * R], U32, name="uq_codes", align_bytes=64)
        uq_scales = keep.tile([P, 4 * R], U8, name="uq_scales", align_bytes=64)
        x_codes = []
        x_scales = []
        for g in range(ROUNDS):
            x_codes.append(keep.tile([P, 4 * P], U32, name="x_codes%d" % g, align_bytes=64))
            x_scales.append(keep.tile([P, 4 * P], U8, name="x_scales%d" % g, align_bytes=64))
        cb_f = keep.tile([P, 32], F32, name="cb_f")
        s0 = keep.tile([P, TILES], F32, name="s0")
        acc = keep.tile([P, TILES], F32, name="acc")
        part = keep.tile([P, TILES], F32, name="part")
        res = keep.tile([P, TILES], F32, name="res")
        fins = []
        a3s = []
        for n in range(FIN_BUFS):
            fins.append(keep.tile([P, 4, 2, R], F32, name="fin%d" % n))
            a3s.append(keep.tile([P, 4, R], F32, name="a3_%d" % n))

        def regroup_u(i):
            nc.vector.tensor_copy(
                out=u_grp[i // 2][:, (i % 2) * D : (i % 2 + 1) * D].rearrange(
                    "p (c i t) -> p c t i", i=4, t=4
                ),
                in_=u_raw[i][:].rearrange("p (t c i) -> p c t i", t=4, i=4),
            )

        def quantise_u(i):
            if i == 0:
                codes, scales = up_codes[:], up_scales[:]
            else:
                codes = uq_codes[:, (i - 2) * R : i * R]
                scales = uq_scales[:, (i - 2) * R : i * R]
            nc.vector.quantize_mx(out=codes.bitcast(FP8X4), scales=scales, in_=u_grp[i // 2][:])

        def spread_constants():
            spread = psum.tile([P, 512], F32, name="spread", tag="for_vector")
            nc.tensor.matmul(out=spread[:, 0:32], lhsT=ones[:], rhs=cb_row[:], start=True, stop=True)
            return spread

        def constants(spread):
            nc.vector.tensor_copy(out=cb_f[:], in_=spread[:, 0:32])

        def mx(bank, t, codes, scales):
            col = (t % 4) * P
            nc.tensor.matmul_mx(
                out=bank,
                lhsT=x_codes[t // 4][:, col : col + P].bitcast(FP8X4),
                lhsT_scale=x_scales[t // 4][:, col : col + P],
                rhs=codes.bitcast(FP8X4),
                rhs_scale=scales,
                start=True,
                stop=True,
            )

        xts = {}
        groupeds = {}

        def transposes(j):
            xt = psum.tile([P, 512], F32, name="xt", tag="for_scalar")
            xts[j] = xt
            for s in range(2):
                x_sb, i = x_of[2 * j + s]
                words = x_sb[:, i, :].bitcast(F32)
                for u in range(2):
                    col = (2 * s + u) * P
                    nc.tensor.transpose(
                        xt[:, col : col + P], words[:, u * P : (u + 1) * P], ident[:]
                    )

        def copy_xt(j):
            if j % 2 == 0:
                grouped = work.tile([P, 2048], BF16, name="grouped", align_bytes=64)
                groupeds[j // 2] = grouped
            half = j % 2
            nc.scalar.copy(
                out=groupeds[j // 2][:, half * 1024 : (half + 1) * 1024]
                .bitcast(F32)
                .rearrange("p (s b u) -> p s b u", s=2, u=2),
                in_=xts[j][:].rearrange("p (s u b) -> p s b u", s=2, u=2),
            )

        def quantise_x(g):
            nc.vector.quantize_mx(
                out=x_codes[g][:].bitcast(FP8X4), scales=x_scales[g][:], in_=groupeds[g][:]
            )

        pbs = {}
        dbs = {}
        qbs = {}
        q4s = {}

        def pass_d1_d3(j):
            pb = psum.tile([P, 512], F32, name="pb", tag="for_scalar")
            pbs[j] = pb
            for s in range(2):
                mx(pb[:, s * 256 : (s + 1) * 256], 2 * j + s, up_codes[:], up_scales[:])

        def pass_d0(g):
            side = "for_vector" if d0_on_vector(g) else "for_scalar"
            db = psum.tile([P, 512], F32, name="db", tag=side)
            dbs[g] = db
            for i in range(4):
                mx(db[:, i * R : (i + 1) * R], 4 * g + i, uq_codes[:, 0:R], uq_scales[:, 0:R])

        def pass_d4(g):
            q4 = psum.tile([P, 512], F32, name="q4", tag="for_vector")
            q4s[g] = q4
            for i in range(4):
                mx(q4[:, i * R : (i + 1) * R], 4 * g + i, uq_codes[:, 384:512], uq_scales[:, 384:512])

        def pass_d2_d5(j):
            qb = psum.tile([P, 512], F32, name="qb", tag="for_vector")
            qbs[j] = qb
            for s in range(2):
                mx(qb[:, s * 256 : (s + 1) * 256], 2 * j + s, uq_codes[:, 128:384], uq_scales[:, 128:384])

        def copies(j):
            pb = pbs[j][:].rearrange("p (s c) -> p s c", s=2)
            n = (j // 2) % FIN_BUFS
            lo = 2 * (j % 2)
            nc.scalar.copy(out=a3s[n][:, lo : lo + 2, :], in_=pb[:, :, 128:256])
            nc.scalar.activation(
                out=fins[n][:, lo : lo + 2, 0, :], in_=pb[:, :, 0:128], func=COPY, scale=cb_f[:, 1:2]
            )

        def linear_sums(g):
            if d0_on_vector(g):
                nc.vector.tensor_reduce(
                    out=s0[:, 4 * g : 4 * g + 4],
                    in_=dbs[g][:].rearrange("p (s r) -> p s r", s=4),
                    op=ADD,
                    axis=mybir.AxisListType.X,
                )
                return
            for i in range(4):
                junk_s = work.tile([P, R], F32, name="junk_s")
                nc.scalar.activation(
                    out=junk_s[:],
                    in_=dbs[g][:, i * R : (i + 1) * R],
                    func=COPY,
                    accum_out=s0[:, 4 * g + i : 4 * g + i + 1],
                )

        def cubic_head(g):
            nc.vector.scalar_tensor_tensor(
                out=fins[g % FIN_BUFS][:, :, 1, :],
                in0=a3s[g % FIN_BUFS][:],
                scalar=cb_f[:, 2:3],
                in1=q4s[g][:].rearrange("p (s r) -> p s r", s=4),
                op0=MULT,
                op1=MULT,
            )

        def sums(t):
            fin = fins[(t // 4) % FIN_BUFS]
            junk_v = work.tile([P, 2 * R], F32, name="junk_v")
            nc.vector.scalar_tensor_tensor(
                out=junk_v[:],
                in0=fin[:, t % 4, :, :].rearrange("p b r -> p (b r)"),
                scalar=1.0,
                in1=qbs[t // 2][:, (t % 2) * 256 : (t % 2 + 1) * 256],
                op0=MULT,
                op1=MULT,
                accum_out=acc[:, t : t + 1],
            )

        regroup_u(0)
        regroup_u(1)
        quantise_u(0)

        for r in range(-X_LEAD, ROUNDS):
            gx, gq, gs = r + X_LEAD, r + Q_LEAD, r + S_LEAD
            if gx < ROUNDS:
                transposes(2 * gx)
                transposes(2 * gx + 1)
                copy_xt(2 * gx)
                copy_xt(2 * gx + 1)
            if gq == 1:
                spread = spread_constants()
                constants(spread)
                regroup_u(4)
                regroup_u(5)
                quantise_u(4)
            side = 0 <= gs < ROUNDS
            if r >= 0:
                pass_d4(r)
            if side:
                pass_d1_d3(2 * gs)
            if r >= 0:
                pass_d2_d5(2 * r)
            if side:
                pass_d1_d3(2 * gs + 1)
            if r >= 0:
                pass_d2_d5(2 * r + 1)
            linear = side and gs < LATE_FROM
            if linear:
                pass_d0(gs)
            if side:
                copies(2 * gs)
                copies(2 * gs + 1)
            for g in LATE_TURNS.get(r, ()):
                pass_d0(g)
                linear_sums(g)
            if r >= 0:
                cubic_head(r)
            if 0 <= gq < ROUNDS:
                quantise_x(gq)
            if gq == 0:
                regroup_u(2)
                regroup_u(3)
                quantise_u(2)
            if r >= 0:
                sums(4 * r)
                sums(4 * r + 1)
                sums(4 * r + 2)
            if linear:
                linear_sums(gs)
            if r == ROUNDS - 1:
                nc.vector.tensor_scalar(
                    out=part[:],
                    in0=s0[:],
                    scalar1=cb_f[:, 0:1],
                    scalar2=cb_f[:, 16:17],
                    op0=MULT,
                    op1=ADD,
                )
            if r >= 0:
                sums(4 * r + 3)

        nc.vector.tensor_tensor(out=res[:], in0=part[:], in1=acc[:], op=ADD)
        nc.sync.dma_start(out=out.rearrange("(p t) -> p t", t=TILES), in_=res[:])
